import numpy as np
import ml_dtypes


def mxq(x, axis, fmt="e4m3"):
    dtype, down = {"e4m3": (ml_dtypes.float8_e4m3fn, 7), "e5m2": (ml_dtypes.float8_e5m2, 14)}[fmt]
    v = np.moveaxis(np.asarray(x, np.float32).astype(ml_dtypes.bfloat16).astype(np.float64), axis, -1)
    blocks = v.reshape(v.shape[:-1] + (-1, 32))
    amax = np.abs(blocks).max(-1, keepdims=True)
    byte = np.maximum(np.where(amax > 0, np.frexp(amax)[1] - 1 + 127, 0) - down, 1)
    scale = np.exp2(byte - 127.0)
    codes = (blocks / scale).astype(np.float32).astype(dtype).astype(np.float64)
    return np.moveaxis((codes * scale).reshape(v.shape), -1, axis)


WIDE = False


def mx_kscale(k):
    if not WIDE:
        return np.ones(k)
    levels = np.array([10, -10, 5, -5, 0])
    if k % 512:
        return np.exp2(np.random.permutation(np.resize(levels, k // 32))).repeat(32)
    a = np.empty((k // 512, 16))
    for p in range(k // 512):
        a[p, :8] = np.random.permutation(np.resize(levels, 8))
        for g in range(8):
            far = levels[np.abs(levels - a[p, g]) >= 10]
            a[p, g + 8] = far[np.random.randint(len(far))]
    return np.exp2(a.ravel()).repeat(32)


BF16 = ml_dtypes.bfloat16


def bf(x):
    return np.asarray(x, np.float32).astype(BF16)


def f64(x):
    return np.asarray(x).astype(np.float64)


B, C, H, W = 1, 512, 32, 32
N = H * W
SIG = 3.0


def setup_inputs():
    s, t = mx_kscale(C), mx_kscale(C)
    r = np.sqrt(SIG / np.sqrt(C))
    return {
        "q_ir": bf(np.random.standard_normal((B, C, N)) * r / t[:, None]),
        "irSegF": bf(np.random.standard_normal((B, C, H, W)) * s[:, None, None]),
        "Wk_dr": bf(np.random.standard_normal((C, C)) * r / np.sqrt(C) * t[:, None] / s[None, :]),
        "bk_dr": bf(np.random.standard_normal(C) * 0.1 * t),
    }


def reference(q_ir, irSegF, Wk_dr, bk_dr):
    seg = f64(irSegF).reshape(B, C, N)
    key = (mxq(f64(Wk_dr), 1, "e4m3") @ mxq(seg, 1, "e4m3")) + f64(bk_dr)[None, :, None]
    s = mxq(f64(q_ir), 1, "e4m3").transpose(0, 2, 1) @ mxq(key, 1, "e4m3")
    e = np.exp(s - s.max(1, keepdims=True))
    return e / e.sum(1, keepdims=True)

@@ -1,0 +1,439 @@
+from contextlib import ExitStack
+
+import concourse.masks as masks
+import concourse.mybir as mybir
+
+F32 = mybir.dt.float32
+BF16 = mybir.dt.bfloat16
+U32 = mybir.dt.uint32
+U8 = mybir.dt.uint8
+FP8X4 = mybir.dt.float8_e4m3fn_x4
+ALU = mybir.AluOpType
+ACT = mybir.ActivationFunctionType
+AX = mybir.AxisListType
+
+KEY_BANK_DT = F32
+
+P = 128
+C = 512
+NQ = 1024
+MK = 1024
+HALF = 512
+
+FLOPS = 2 * C * C * MK + 2 * NQ * MK * C
+
+
+def tile_featuremaptransformer_pb_kernel(tc, q_ir, irSegF, Wk_dr, bk_dr, out):
+    nc = tc.nc
+    views = {
+        "q": q_ir[0].rearrange("(p j) n -> p j n", j=4),
+        "s": irSegF[0].rearrange("(p j) h w -> p j (h w)", j=4),
+    }
+    w_v = Wk_dr.rearrange("(m t) c -> m t c", t=4)
+    b_v = bk_dr.rearrange("(p t) -> p t", t=4)
+    out_v = out[0].rearrange("(k p) m -> p k m", p=P)
+
+    with ExitStack() as ctx:
+        keep = ctx.enter_context(tc.tile_pool(name="keep", bufs=1))
+        work = ctx.enter_context(tc.tile_pool(name="work", bufs=4))
+        psum = ctx.enter_context(tc.psum_pool(name="psum", bufs=2))
+        ctx.enter_context(tc.manual_schedule())
+        raws = {}
+        w_raw = {}
+        b_sb = keep.tile([P, 4], BF16, name="b_sb", tag="b_sb")
+        ident = keep.tile([P, P], F32, name="ident", tag="ident")
+        w_codes = keep.tile([P, C], U32, name="w_codes", tag="w_codes", align_bytes=64)
+        w_scales = keep.tile([P, C], U8, name="w_scales", tag="w_scales", align_bytes=64)
+        wg = keep.tile([P, 4 * C], BF16, name="wg", tag="wg", align_bytes=64)
+        wg_words = wg[:].bitcast(F32)
+        codes = {}
+        scales = {}
+        grouped = {}
+        for kind in ("q", "s"):
+            codes[kind] = keep.tile([P, 1024], U32, name="codes_" + kind, tag="codes_" + kind, align_bytes=64)
+            scales[kind] = keep.tile([P, 1024], U8, name="scales_" + kind, tag="scales_" + kind, align_bytes=64)
+            grouped[kind] = keep.tile([P, 1024, 4], BF16, name="gr_" + kind, tag="gr_" + kind, align_bytes=64)
+        wt = {}
+        keyb = {}
+        kgs = {}
+        kcodes = {}
+        s_banks = {}
+        nmxs = {}
+        mx2s = {}
+        es = {}
+        sms = {}
+        rs = {}
+        ens = {}
+        trs = {}
+        osb = {}
+
+        def load(kind, a=0, b=0):
+            if kind == "b":
+                nc.scalar.dma_start(out=b_sb[:], in_=b_v)
+            elif kind == "w":
+                raw = keep.tile([P, 2, C], BF16, name="w_raw%d" % a, tag="w_raw%d" % a)
+                nc.sync.dma_start(out=raw[:], in_=w_v[:, 2 * a:2 * a + 2, :])
+                w_raw[a] = raw
+            else:
+                raw = keep.tile([P, 4, b - a], BF16, name="raw_%s%d" % (kind, a), tag="raw_%s%d" % (kind, a))
+                nc.sync.dma_start(out=raw[:], in_=views[kind][:, :, a:b])
+                raws[(kind, a, b)] = raw
+
+        def tab():
+            zero = keep.tile([P, 1], F32, name="zero", tag="zero")
+            junk = keep.tile([P, 1], F32, name="junk", tag="junk")
+            nc.vector.memset(zero[:], 0.0)
+            nc.scalar.activation(out=junk[:], in_=zero[:], func=ACT.Exp)
+
+        def mkident():
+            masks.make_identity(nc, ident[:])
+
+        def tw(g):
+            wt_ps = psum.tile([P, 2, 2, P], F32, name="wt_ps", tag="tr", bufs=3)
+            words = w_raw[g][:].rearrange("p t c -> p (t c)").bitcast(F32)
+            for tt in range(2):
+                for u in range(2):
+                    nc.tensor.transpose(wt_ps[:, tt, u, :], words[:, 256 * tt + u:256 * (tt + 1):2], ident[:])
+            wt[g] = wt_ps
+
+        def cow(g, eng):
+            dst = wg_words[:, 512 * g:512 * (g + 1)].rearrange("p (tt m u) -> p tt m u", tt=2, u=2)
+            srcp = wt[g][:].rearrange("p tt u m -> p tt m u")
+            if eng == "V":
+                nc.vector.tensor_copy(out=dst, in_=srcp)
+            else:
+                nc.scalar.copy(out=dst, in_=srcp)
+
+        def qw(g):
+            nc.vector.quantize_mx(
+                out=w_codes[:, 256 * g:256 * (g + 1)].bitcast(FP8X4),
+                scales=w_scales[:, 256 * g:256 * (g + 1)],
+                in_=wg[:, 1024 * g:1024 * (g + 1)],
+            )
+
+        def il(kind, a, b, eng):
+            srcr = None
+            for key in raws:
+                if key[0] == kind and key[1] <= a and b <= key[2]:
+                    srcr = raws[key][:, :, a - key[1]:b - key[1]].rearrange("p j w -> p w j")
+            dst = grouped[kind][:, a:b, :]
+            if eng == "V":
+                nc.vector.tensor_copy(out=dst, in_=srcr)
+            elif eng == "S":
+                nc.scalar.copy(out=dst, in_=srcr)
+            else:
+                nc.gpsimd.tensor_scalar(out=dst, in0=srcr, scalar1=1.0, scalar2=0.0, op0=ALU.mult, op1=ALU.add)
+
+        def qz(kind, a, b):
+            nc.vector.quantize_mx(
+                out=codes[kind][:, a:b].bitcast(FP8X4),
+                scales=scales[kind][:, a:b],
+                in_=grouped[kind][:, a:b, :].rearrange("p w j -> p (w j)"),
+            )
+
+        def st1(j):
+            key_ps = psum.tile([P, 4, P], KEY_BANK_DT, name="key_ps", tag="key", bufs=1)
+            cols = slice(j * P, (j + 1) * P)
+            for t in range(4):
+                nc.tensor.matmul_mx(
+                    out=key_ps[:, t, :],
+                    lhsT=w_codes[:, t * P:(t + 1) * P].bitcast(FP8X4),
+                    lhsT_scale=w_scales[:, t * P:(t + 1) * P],
+                    rhs=codes["s"][:, cols].bitcast(FP8X4),
+                    rhs_scale=scales["s"][:, cols],
+                    start=True,
+                    stop=True,
+                )
+            keyb[j] = key_ps
+
+        def add(j):
+            kg = work.tile([P, P, 4], BF16, name="kg", tag="kg", align_bytes=64)
+            nc.vector.tensor_tensor(
+                out=kg[:],
+                in0=keyb[j][:].rearrange("p t n -> p n t"),
+                in1=b_sb[:].unsqueeze(1).to_broadcast([P, P, 4]),
+                op=ALU.add,
+            )
+            kgs[j] = kg
+
+        def qk(j):
+            kc = work.tile([P, P], U32, name="kc", tag="kc", align_bytes=64)
+            ks = work.tile([P, P], U8, name="ks", tag="ks", align_bytes=64)
+            nc.vector.quantize_mx(out=kc[:].bitcast(FP8X4), scales=ks[:], in_=kgs[j][:].rearrange("p n t -> p (n t)"))
+            kcodes[j] = (kc, ks)
+
+        def sc(j, h):
+            kc, ks = kcodes[j]
+            s_ps = psum.tile([P, HALF], F32, name="s_ps", tag="s", bufs=4)
+            cols = slice(h * HALF, (h + 1) * HALF)
+            nc.tensor.matmul_mx(
+                out=s_ps[:],
+                lhsT=kc[:].bitcast(FP8X4),
+                lhsT_scale=ks[:],
+                rhs=codes["q"][:, cols].bitcast(FP8X4),
+                rhs_scale=scales["q"][:, cols],
+                start=True,
+                stop=True,
+            )
+            s_banks[(j, h)] = s_ps
+
+        def mx(j, h):
+            if h == 0:
+                mx2 = work.tile([P, 2], F32, name="mx2", tag="mx2")
+                mx2s[j] = mx2
+            nc.vector.reduce_max(out=mx2s[j][:, h:h + 1], in_=s_banks[(j, h)][:], axis=AX.X)
+
+        def nmx(j):
+            neg = work.tile([P, 1], F32, name="neg", tag="neg")
+            nc.vector.tensor_scalar(out=neg[:], in0=mx2s[j][:, 0:1], scalar1=mx2s[j][:, 1:2], scalar2=-1.0, op0=ALU.max, op1=ALU.mult)
+            nmxs[j] = neg
+
+        def ex(j, h):
+            if h == 0:
+                e = work.tile([P, NQ], F32, name="e", tag="e")
+                sm2 = work.tile([P, 2], F32, name="sm2", tag="sm2")
+                es[j] = e
+                sms[j] = sm2
+            nc.scalar.activation(
+                out=es[j][:, h * HALF:(h + 1) * HALF],
+                in_=s_banks[(j, h)][:],
+                func=ACT.Exp,
+                bias=nmxs[j][:, 0:1],
+                scale=1.0,
+                accum_out=sms[j][:, h:h + 1],
+            )
+
+        def rc(j):
+            tot = work.tile([P, 1], F32, name="tot", tag="tot")
+            r = work.tile([P, 1], F32, name="r", tag="r")
+            nc.vector.tensor_scalar(out=tot[:], in0=sms[j][:, 0:1], scalar1=sms[j][:, 1:2], scalar2=None, op0=ALU.add)
+            nc.vector.reciprocal(out=r[:], in_=tot[:])
+            rs[j] = r
+            en = work.tile([P, NQ], F32, name="en", tag="en")
+            ens[j] = en
+
+        def nm(j, a, b, eng):
+            dst = ens[j][:, a:b]
+            srce = es[j][:, a:b]
+            if eng == "V":
+                nc.vector.tensor_scalar(out=dst, in0=srce, scalar1=rs[j][:, 0:1], scalar2=None, op0=ALU.mult)
+            elif eng == "G":
+                nc.gpsimd.tensor_scalar(out=dst, in0=srce, scalar1=rs[j][:, 0:1], scalar2=0.0, op0=ALU.mult, op1=ALU.add)
+            else:
+                nc.scalar.activation(out=dst, in_=srce, func=ACT.Copy, scale=rs[j][:, 0:1])
+
+        def tr(j, g):
+            tr_ps = psum.tile([P, 4, P], F32, name="tr_ps", tag="tr", bufs=3)
+            for b in range(4):
+                k = 4 * g + b
+                nc.tensor.transpose(tr_ps[:, b, :], ens[j][:, k * P:(k + 1) * P], ident[:])
+            trs[(j, g)] = tr_ps
+
+        def co(j, g, eng):
+            o_sb = work.tile([P, 4, P], F32, name="o_sb", tag="o_sb", bufs=8)
+            if eng == "V":
+                nc.vector.tensor_copy(out=o_sb[:], in_=trs[(j, g)][:])
+            else:
+                nc.scalar.copy(out=o_sb[:], in_=trs[(j, g)][:])
+            osb[(j, g)] = o_sb
+
+        def st(j, g):
+            nc.sync.dma_start(out=out_v[:, 4 * g:4 * g + 4, j * P:(j + 1) * P], in_=osb[(j, g)][:])
+
+        load("b")
+        load("w", 0)
+        load("w", 1)
+        load("s", 0, 256)
+        load("q", 0, 512)
+        load("q", 512, 1024)
+        load("s", 256, 512)
+        load("s", 512, 1024)
+        tab()
+        mkident()
+        tw(0)
+        cow(0, "V")
+        tw(1)
+        cow(1, "S")
+        il("s", 0, 256, "V")
+        qw(0)
+        qw(1)
+        qz("s", 0, 256)
+        il("q", 256, 512, "S")
+        il("q", 0, 256, "V")
+        st1(0)
+        add(0)
+        il("q", 768, 1024, "S")
+        il("q", 512, 768, "V")
+        qk(0)
+        qz("q", 0, 512)
+        sc(0, 0)
+        st1(1)
+        qz("q", 512, 1024)
+        sc(0, 1)
+        il("s", 256, 512, "S")
+        il("s", 512, 768, "S")
+        mx(0, 0)
+        mx(0, 1)
+        nmx(0)
+        ex(0, 0)
+        ex(0, 1)
+        qz("s", 256, 512)
+        add(1)
+        qk(1)
+        il("s", 768, 1024, "S")
+        st1(2)
+        sc(1, 0)
+        sc(1, 1)
+        add(2)
+        qk(2)
+        mx(1, 0)
+        mx(1, 1)
+        nmx(1)
+        ex(1, 0)
+        ex(1, 1)
+        st1(3)
+        sc(2, 0)
+        sc(2, 1)
+        add(3)
+        qz("s", 512, 1024)
+        rc(0)
+        qk(3)
+        nm(0, 0, 256, "G")
+        nm(0, 256, 512, "G")
+        nm(0, 512, 768, "G")
+        nm(0, 768, 1024, "G")
+        mx(2, 0)
+        mx(2, 1)
+        nmx(2)
+        ex(2, 0)
+        ex(2, 1)
+        st1(4)
+        sc(3, 0)
+        sc(3, 1)
+        add(4)
+        rc(1)
+        qk(4)
+        nm(1, 0, 256, "G")
+        nm(1, 256, 512, "G")
+        nm(1, 512, 768, "G")
+        nm(1, 768, 1024, "G")
+        tr(0, 0)
+        co(0, 0, "S")
+        st(0, 0)
+        tr(0, 1)
+        co(0, 1, "S")
+        st(0, 1)
+        mx(3, 0)
+        mx(3, 1)
+        nmx(3)
+        ex(3, 0)
+        ex(3, 1)
+        st1(5)
+        sc(4, 0)
+        sc(4, 1)
+        add(5)
+        rc(2)
+        qk(5)
+        nm(2, 0, 256, "G")
+        nm(2, 256, 512, "G")
+        nm(2, 512, 768, "G")
+        nm(2, 768, 1024, "G")
+        tr(1, 0)
+        co(1, 0, "S")
+        st(1, 0)
+        tr(1, 1)
+        co(1, 1, "S")
+        st(1, 1)
+        mx(4, 0)
+        mx(4, 1)
+        nmx(4)
+        ex(4, 0)
+        ex(4, 1)
+        st1(6)
+        sc(5, 0)
+        sc(5, 1)
+        add(6)
+        rc(3)
+        qk(6)
+        nm(3, 0, 256, "G")
+        nm(3, 256, 512, "G")
+        nm(3, 512, 768, "G")
+        nm(3, 768, 1024, "G")
+        tr(2, 0)
+        co(2, 0, "S")
+        st(2, 0)
+        tr(2, 1)
+        co(2, 1, "S")
+        st(2, 1)
+        mx(5, 0)
+        mx(5, 1)
+        nmx(5)
+        ex(5, 0)
+        ex(5, 1)
+        st1(7)
+        sc(6, 0)
+        sc(6, 1)
+        add(7)
+        rc(4)
+        qk(7)
+        nm(4, 0, 256, "G")
+        nm(4, 256, 512, "G")
+        nm(4, 512, 768, "G")
+        nm(4, 768, 1024, "G")
+        tr(3, 0)
+        co(3, 0, "S")
+        st(3, 0)
+        tr(3, 1)
+        co(3, 1, "S")
+        st(3, 1)
+        mx(6, 0)
+        mx(6, 1)
+        nmx(6)
+        ex(6, 0)
+        ex(6, 1)
+        sc(7, 0)
+        sc(7, 1)
+        rc(5)
+        nm(5, 0, 256, "G")
+        nm(5, 256, 512, "G")
+        nm(5, 512, 768, "G")
+        nm(5, 768, 1024, "G")
+        tr(4, 0)
+        tr(4, 1)
+        mx(7, 0)
+        mx(7, 1)
+        nmx(7)
+        ex(7, 0)
+        ex(7, 1)
+        co(4, 0, "V")
+        st(4, 0)
+        rc(6)
+        nm(6, 0, 256, "G")
+        nm(6, 256, 512, "G")
+        nm(6, 512, 768, "G")
+        nm(6, 768, 1024, "G")
+        co(4, 1, "V")
+        st(4, 1)
+        tr(5, 0)
+        co(5, 0, "S")
+        st(5, 0)
+        tr(5, 1)
+        co(5, 1, "S")
+        st(5, 1)
+        rc(7)
+        nm(7, 0, 256, "V")
+        nm(7, 256, 512, "V")
+        nm(7, 512, 768, "V")
+        nm(7, 768, 1024, "V")
+        tr(6, 0)
+        co(6, 0, "S")
+        st(6, 0)
+        tr(7, 0)
+        co(7, 0, "V")
+        st(7, 0)
+        tr(6, 1)
+        co(6, 1, "S")
+        st(6, 1)
+        tr(7, 1)
+        co(7, 1, "V")
+        st(7, 1)

@@ -115,8 +115,8 @@ def tile_featuremaptransformer_pb_kernel(tc, q_ir, irSegF, Wk_dr, bk_dr, out):
             srcr = None
             for key in raws:
                 if key[0] == kind and key[1] <= a and b <= key[2]:
-                    srcr = raws[key][:, :, a - key[1]:b - key[1]].rearrange("p j w -> p w j")
-            dst = grouped[kind][:, a:b, :]
+                    srcr = raws[key][:, :, a - key[1]:b - key[1]].rearrange("p j (c i) -> p c j i", i=4)
+            dst = grouped[kind][:, a:b, :].rearrange("p (c i) j -> p c j i", i=4)
             if eng == "V":
                 nc.vector.tensor_copy(out=dst, in_=srcr)
             elif eng == "S":
@@ -181,11 +181,11 @@ def tile_featuremaptransformer_pb_kernel(tc, q_ir, irSegF, Wk_dr, bk_dr, out):
             if h == 0:
                 mx2 = work.tile([P, 2], F32, name="mx2", tag="mx2")
                 mx2s[j] = mx2
-            nc.vector.reduce_max(out=mx2s[j][:, h:h + 1], in_=s_banks[(j, h)][:], axis=AX.X)
+            nc.vector.tensor_reduce(out=mx2s[j][:, h:h + 1], in_=s_banks[(j, h)][:], axis=AX.X, op=ALU.max, negate=True)
 
         def nmx(j):
             neg = work.tile([P, 1], F32, name="neg", tag="neg")
-            nc.vector.tensor_scalar(out=neg[:], in0=mx2s[j][:, 0:1], scalar1=mx2s[j][:, 1:2], scalar2=-1.0, op0=ALU.max, op1=ALU.mult)
+            nc.vector.tensor_reduce(out=neg[:], in_=mx2s[j][:], axis=AX.X, op=ALU.min)
             nmxs[j] = neg
 
         def ex(j, h):
@@ -206,7 +206,7 @@ def tile_featuremaptransformer_pb_kernel(tc, q_ir, irSegF, Wk_dr, bk_dr, out):
         def rc(j):
             tot = work.tile([P, 1], F32, name="tot", tag="tot")
             r = work.tile([P, 1], F32, name="r", tag="r")
-            nc.vector.tensor_scalar(out=tot[:], in0=sms[j][:, 0:1], scalar1=sms[j][:, 1:2], scalar2=None, op0=ALU.add)
+            nc.vector.tensor_reduce(out=tot[:], in_=sms[j][:], axis=AX.X, op=ALU.add)
             nc.vector.reciprocal(out=r[:], in_=tot[:])
             rs[j] = r
             en = work.tile([P, NQ], F32, name="en", tag="en")
@@ -251,7 +251,7 @@ def tile_featuremaptransformer_pb_kernel(tc, q_ir, irSegF, Wk_dr, bk_dr, out):
         tab()
         mkident()
         tw(0)
-        cow(0, "V")
+        cow(0, "S")
         tw(1)
         cow(1, "S")
         il("s", 0, 256, "V")
@@ -298,10 +298,8 @@ def tile_featuremaptransformer_pb_kernel(tc, q_ir, irSegF, Wk_dr, bk_dr, out):
         qz("s", 512, 1024)
         rc(0)
         qk(3)
-        nm(0, 0, 256, "G")
-        nm(0, 256, 512, "G")
-        nm(0, 512, 768, "G")
-        nm(0, 768, 1024, "G")
+        nm(0, 0, 512, "G")
+        nm(0, 512, 1024, "G")
         mx(2, 0)
         mx(2, 1)
         nmx(2)
@@ -313,10 +311,8 @@ def tile_featuremaptransformer_pb_kernel(tc, q_ir, irSegF, Wk_dr, bk_dr, out):
         add(4)
         rc(1)
         qk(4)
-        nm(1, 0, 256, "G")
-        nm(1, 256, 512, "G")
-        nm(1, 512, 768, "G")
-        nm(1, 768, 1024, "G")
+        nm(1, 0, 512, "G")
+        nm(1, 512, 1024, "G")
         tr(0, 0)
         co(0, 0, "S")
         st(0, 0)
@@ -334,10 +330,8 @@ def tile_featuremaptransformer_pb_kernel(tc, q_ir, irSegF, Wk_dr, bk_dr, out):
         add(5)
         rc(2)
         qk(5)
-        nm(2, 0, 256, "G")
-        nm(2, 256, 512, "G")
-        nm(2, 512, 768, "G")
-        nm(2, 768, 1024, "G")
+        nm(2, 0, 512, "G")
+        nm(2, 512, 1024, "G")
         tr(1, 0)
         co(1, 0, "S")
         st(1, 0)
@@ -355,10 +349,8 @@ def tile_featuremaptransformer_pb_kernel(tc, q_ir, irSegF, Wk_dr, bk_dr, out):
         add(6)
         rc(3)
         qk(6)
-        nm(3, 0, 256, "G")
-        nm(3, 256, 512, "G")
-        nm(3, 512, 768, "G")
-        nm(3, 768, 1024, "G")
+        nm(3, 0, 512, "G")
+        nm(3, 512, 1024, "G")
         tr(2, 0)
         co(2, 0, "S")
         st(2, 0)
@@ -376,10 +368,8 @@ def tile_featuremaptransformer_pb_kernel(tc, q_ir, irSegF, Wk_dr, bk_dr, out):
         add(7)
         rc(4)
         qk(7)
-        nm(4, 0, 256, "G")
-        nm(4, 256, 512, "G")
-        nm(4, 512, 768, "G")
-        nm(4, 768, 1024, "G")
+        nm(4, 0, 512, "G")
+        nm(4, 512, 1024, "G")
         tr(3, 0)
         co(3, 0, "S")
         st(3, 0)
@@ -394,10 +384,8 @@ def tile_featuremaptransformer_pb_kernel(tc, q_ir, irSegF, Wk_dr, bk_dr, out):
         sc(7, 0)
         sc(7, 1)
         rc(5)
-        nm(5, 0, 256, "G")
-        nm(5, 256, 512, "G")
-        nm(5, 512, 768, "G")
-        nm(5, 768, 1024, "G")
+        nm(5, 0, 512, "G")
+        nm(5, 512, 1024, "G")
         tr(4, 0)
         tr(4, 1)
         mx(7, 0)
@@ -408,10 +396,8 @@ def tile_featuremaptransformer_pb_kernel(tc, q_ir, irSegF, Wk_dr, bk_dr, out):
         co(4, 0, "V")
         st(4, 0)
         rc(6)
-        nm(6, 0, 256, "G")
-        nm(6, 256, 512, "G")
-        nm(6, 512, 768, "G")
-        nm(6, 768, 1024, "G")
+        nm(6, 0, 512, "G")
+        nm(6, 512, 1024, "G")
         co(4, 1, "V")
         st(4, 1)
         tr(5, 0)

@@ -298,8 +298,8 @@ def tile_featuremaptransformer_pb_kernel(tc, q_ir, irSegF, Wk_dr, bk_dr, out):
         qz("s", 512, 1024)
         rc(0)
         qk(3)
-        nm(0, 0, 512, "G")
-        nm(0, 512, 1024, "G")
+        nm(0, 0, 512, "V")
+        nm(0, 512, 1024, "V")
         mx(2, 0)
         mx(2, 1)
         nmx(2)
@@ -311,8 +311,8 @@ def tile_featuremaptransformer_pb_kernel(tc, q_ir, irSegF, Wk_dr, bk_dr, out):
         add(4)
         rc(1)
         qk(4)
-        nm(1, 0, 512, "G")
-        nm(1, 512, 1024, "G")
+        nm(1, 0, 512, "V")
+        nm(1, 512, 1024, "V")
         tr(0, 0)
         co(0, 0, "S")
         st(0, 0)
@@ -330,8 +330,8 @@ def tile_featuremaptransformer_pb_kernel(tc, q_ir, irSegF, Wk_dr, bk_dr, out):
         add(5)
         rc(2)
         qk(5)
-        nm(2, 0, 512, "G")
-        nm(2, 512, 1024, "G")
+        nm(2, 0, 512, "V")
+        nm(2, 512, 1024, "V")
         tr(1, 0)
         co(1, 0, "S")
         st(1, 0)
@@ -349,8 +349,8 @@ def tile_featuremaptransformer_pb_kernel(tc, q_ir, irSegF, Wk_dr, bk_dr, out):
         add(6)
         rc(3)
         qk(6)
-        nm(3, 0, 512, "G")
-        nm(3, 512, 1024, "G")
+        nm(3, 0, 512, "V")
+        nm(3, 512, 1024, "V")
         tr(2, 0)
         co(2, 0, "S")
         st(2, 0)
@@ -368,8 +368,8 @@ def tile_featuremaptransformer_pb_kernel(tc, q_ir, irSegF, Wk_dr, bk_dr, out):
         add(7)
         rc(4)
         qk(7)
-        nm(4, 0, 512, "G")
-        nm(4, 512, 1024, "G")
+        nm(4, 0, 512, "V")
+        nm(4, 512, 1024, "V")
         tr(3, 0)
         co(3, 0, "S")
         st(3, 0)
@@ -384,8 +384,8 @@ def tile_featuremaptransformer_pb_kernel(tc, q_ir, irSegF, Wk_dr, bk_dr, out):
         sc(7, 0)
         sc(7, 1)
         rc(5)
-        nm(5, 0, 512, "G")
-        nm(5, 512, 1024, "G")
+        nm(5, 0, 512, "V")
+        nm(5, 512, 1024, "V")
         tr(4, 0)
         tr(4, 1)
         mx(7, 0)
@@ -396,8 +396,8 @@ def tile_featuremaptransformer_pb_kernel(tc, q_ir, irSegF, Wk_dr, bk_dr, out):
         co(4, 0, "V")
         st(4, 0)
         rc(6)
-        nm(6, 0, 512, "G")
-        nm(6, 512, 1024, "G")
+        nm(6, 0, 512, "V")
+        nm(6, 512, 1024, "V")
         co(4, 1, "V")
         st(4, 1)
         tr(5, 0)

from contextlib import ExitStack

import concourse.masks as masks
import concourse.mybir as mybir

F32 = mybir.dt.float32
BF16 = mybir.dt.bfloat16
U32 = mybir.dt.uint32
U8 = mybir.dt.uint8
FP8X4 = mybir.dt.float8_e4m3fn_x4
ALU = mybir.AluOpType
ACT = mybir.ActivationFunctionType
AX = mybir.AxisListType

KEY_BANK_DT = F32

P = 128
C = 512
NQ = 1024
MK = 1024
HALF = 512

FLOPS = 2 * C * C * MK + 2 * NQ * MK * C


def tile_featuremaptransformer_pb_kernel(tc, q_ir, irSegF, Wk_dr, bk_dr, out):
    nc = tc.nc
    views = {
        "q": q_ir[0].rearrange("(p j) n -> p j n", j=4),
        "s": irSegF[0].rearrange("(p j) h w -> p j (h w)", j=4),
    }
    w_v = Wk_dr.rearrange("(m t) c -> m t c", t=4)
    b_v = bk_dr.rearrange("(p t) -> p t", t=4)
    out_v = out[0].rearrange("(k p) m -> p k m", p=P)

    with ExitStack() as ctx:
        keep = ctx.enter_context(tc.tile_pool(name="keep", bufs=1))
        work = ctx.enter_context(tc.tile_pool(name="work", bufs=4))
        psum = ctx.enter_context(tc.psum_pool(name="psum", bufs=2))
        ctx.enter_context(tc.manual_schedule())
        raws = {}
        w_raw = {}
        b_sb = keep.tile([P, 4], BF16, name="b_sb", tag="b_sb")
        ident = keep.tile([P, P], F32, name="ident", tag="ident")
        w_codes = keep.tile([P, C], U32, name="w_codes", tag="w_codes", align_bytes=64)
        w_scales = keep.tile([P, C], U8, name="w_scales", tag="w_scales", align_bytes=64)
        wg = keep.tile([P, 4 * C], BF16, name="wg", tag="wg", align_bytes=64)
        wg_words = wg[:].bitcast(F32)
        codes = {}
        scales = {}
        grouped = {}
        for kind in ("q", "s"):
            codes[kind] = keep.tile([P, 1024], U32, name="codes_" + kind, tag="codes_" + kind, align_bytes=64)
            scales[kind] = keep.tile([P, 1024], U8, name="scales_" + kind, tag="scales_" + kind, align_bytes=64)
            grouped[kind] = keep.tile([P, 1024, 4], BF16, name="gr_" + kind, tag="gr_" + kind, align_bytes=64)
        wt = {}
        keyb = {}
        kgs = {}
        kcodes = {}
        s_banks = {}
        nmxs = {}
        mx2s = {}
        es = {}
        sms = {}
        rs = {}
        ens = {}
        trs = {}
        osb = {}

        def load(kind, a=0, b=0):
            if kind == "b":
                nc.scalar.dma_start(out=b_sb[:], in_=b_v)
            elif kind == "w":
                raw = keep.tile([P, 2, C], BF16, name="w_raw%d" % a, tag="w_raw%d" % a)
                nc.sync.dma_start(out=raw[:], in_=w_v[:, 2 * a:2 * a + 2, :])
                w_raw[a] = raw
            else:
                raw = keep.tile([P, 4, b - a], BF16, name="raw_%s%d" % (kind, a), tag="raw_%s%d" % (kind, a))
                nc.sync.dma_start(out=raw[:], in_=views[kind][:, :, a:b])
                raws[(kind, a, b)] = raw

        def tab():
            zero = keep.tile([P, 1], F32, name="zero", tag="zero")
            junk = keep.tile([P, 1], F32, name="junk", tag="junk")
            nc.vector.memset(zero[:], 0.0)
            nc.scalar.activation(out=junk[:], in_=zero[:], func=ACT.Exp)

        def mkident():
            masks.make_identity(nc, ident[:])

        def tw(g):
            wt_ps = psum.tile([P, 2, 2, P], F32, name="wt_ps", tag="tr", bufs=3)
            words = w_raw[g][:].rearrange("p t c -> p (t c)").bitcast(F32)
            for tt in range(2):
                for u in range(2):
                    nc.tensor.transpose(wt_ps[:, tt, u, :], words[:, 256 * tt + u:256 * (tt + 1):2], ident[:])
            wt[g] = wt_ps

        def cow(g, eng):
            dst = wg_words[:, 512 * g:512 * (g + 1)].rearrange("p (tt m u) -> p tt m u", tt=2, u=2)
            srcp = wt[g][:].rearrange("p tt u m -> p tt m u")
            if eng == "V":
                nc.vector.tensor_copy(out=dst, in_=srcp)
            else:
                nc.scalar.copy(out=dst, in_=srcp)

        def qw(g):
            nc.vector.quantize_mx(
                out=w_codes[:, 256 * g:256 * (g + 1)].bitcast(FP8X4),
                scales=w_scales[:, 256 * g:256 * (g + 1)],
                in_=wg[:, 1024 * g:1024 * (g + 1)],
            )

        def il(kind, a, b, eng):
            srcr = None
            for key in raws:
                if key[0] == kind and key[1] <= a and b <= key[2]:
                    srcr = raws[key][:, :, a - key[1]:b - key[1]].rearrange("p j (c i) -> p c j i", i=4)
            dst = grouped[kind][:, a:b, :].rearrange("p (c i) j -> p c j i", i=4)
            if eng == "V":
                nc.vector.tensor_copy(out=dst, in_=srcr)
            elif eng == "S":
                nc.scalar.copy(out=dst, in_=srcr)
            else:
                nc.gpsimd.tensor_scalar(out=dst, in0=srcr, scalar1=1.0, scalar2=0.0, op0=ALU.mult, op1=ALU.add)

        def qz(kind, a, b):
            nc.vector.quantize_mx(
                out=codes[kind][:, a:b].bitcast(FP8X4),
                scales=scales[kind][:, a:b],
                in_=grouped[kind][:, a:b, :].rearrange("p w j -> p (w j)"),
            )

        def st1(j):
            key_ps = psum.tile([P, 4, P], KEY_BANK_DT, name="key_ps", tag="key", bufs=1)
            cols = slice(j * P, (j + 1) * P)
            for t in range(4):
                nc.tensor.matmul_mx(
                    out=key_ps[:, t, :],
                    lhsT=w_codes[:, t * P:(t + 1) * P].bitcast(FP8X4),
                    lhsT_scale=w_scales[:, t * P:(t + 1) * P],
                    rhs=codes["s"][:, cols].bitcast(FP8X4),
                    rhs_scale=scales["s"][:, cols],
                    start=True,
                    stop=True,
                )
            keyb[j] = key_ps

        def add(j):
            kg = work.tile([P, P, 4], BF16, name="kg", tag="kg", align_bytes=64)
            nc.vector.tensor_tensor(
                out=kg[:],
                in0=keyb[j][:].rearrange("p t n -> p n t"),
                in1=b_sb[:].unsqueeze(1).to_broadcast([P, P, 4]),
                op=ALU.add,
            )
            kgs[j] = kg

        def qk(j):
            kc = work.tile([P, P], U32, name="kc", tag="kc", align_bytes=64)
            ks = work.tile([P, P], U8, name="ks", tag="ks", align_bytes=64)
            nc.vector.quantize_mx(out=kc[:].bitcast(FP8X4), scales=ks[:], in_=kgs[j][:].rearrange("p n t -> p (n t)"))
            kcodes[j] = (kc, ks)

        def sc(j, h):
            kc, ks = kcodes[j]
            s_ps = psum.tile([P, HALF], F32, name="s_ps", tag="s", bufs=4)
            cols = slice(h * HALF, (h + 1) * HALF)
            nc.tensor.matmul_mx(
                out=s_ps[:],
                lhsT=kc[:].bitcast(FP8X4),
                lhsT_scale=ks[:],
                rhs=codes["q"][:, cols].bitcast(FP8X4),
                rhs_scale=scales["q"][:, cols],
                start=True,
                stop=True,
            )
            s_banks[(j, h)] = s_ps

        def mx(j, h):
            if h == 0:
                mx2 = work.tile([P, 2], F32, name="mx2", tag="mx2")
                mx2s[j] = mx2
            nc.vector.tensor_reduce(out=mx2s[j][:, h:h + 1], in_=s_banks[(j, h)][:], axis=AX.X, op=ALU.max, negate=True)

        def nmx(j):
            neg = work.tile([P, 1], F32, name="neg", tag="neg")
            nc.vector.tensor_reduce(out=neg[:], in_=mx2s[j][:], axis=AX.X, op=ALU.min)
            nmxs[j] = neg

        def ex(j, h):
            if h == 0:
                e = work.tile([P, NQ], F32, name="e", tag="e")
                sm2 = work.tile([P, 2], F32, name="sm2", tag="sm2")
                es[j] = e
                sms[j] = sm2
            nc.scalar.activation(
                out=es[j][:, h * HALF:(h + 1) * HALF],
                in_=s_banks[(j, h)][:],
                func=ACT.Exp,
                bias=nmxs[j][:, 0:1],
                scale=1.0,
                accum_out=sms[j][:, h:h + 1],
            )

        def rc(j):
            tot = work.tile([P, 1], F32, name="tot", tag="tot")
            r = work.tile([P, 1], F32, name="r", tag="r")
            nc.vector.tensor_reduce(out=tot[:], in_=sms[j][:], axis=AX.X, op=ALU.add)
            nc.vector.reciprocal(out=r[:], in_=tot[:])
            rs[j] = r
            en = work.tile([P, NQ], F32, name="en", tag="en")
            ens[j] = en

        def nm(j, a, b, eng):
            dst = ens[j][:, a:b]
            srce = es[j][:, a:b]
            if eng == "V":
                nc.vector.tensor_scalar(out=dst, in0=srce, scalar1=rs[j][:, 0:1], scalar2=None, op0=ALU.mult)
            elif eng == "G":
                nc.gpsimd.tensor_scalar(out=dst, in0=srce, scalar1=rs[j][:, 0:1], scalar2=0.0, op0=ALU.mult, op1=ALU.add)
            else:
                nc.scalar.activation(out=dst, in_=srce, func=ACT.Copy, scale=rs[j][:, 0:1])

        def tr(j, g):
            tr_ps = psum.tile([P, 4, P], F32, name="tr_ps", tag="tr", bufs=3)
            for b in range(4):
                k = 4 * g + b
                nc.tensor.transpose(tr_ps[:, b, :], ens[j][:, k * P:(k + 1) * P], ident[:])
            trs[(j, g)] = tr_ps

        def co(j, g, eng):
            o_sb = work.tile([P, 4, P], F32, name="o_sb", tag="o_sb", bufs=8)
            if eng == "V":
                nc.vector.tensor_copy(out=o_sb[:], in_=trs[(j, g)][:])
            else:
                nc.scalar.copy(out=o_sb[:], in_=trs[(j, g)][:])
            osb[(j, g)] = o_sb

        def st(j, g):
            nc.sync.dma_start(out=out_v[:, 4 * g:4 * g + 4, j * P:(j + 1) * P], in_=osb[(j, g)][:])

        load("b")
        load("w", 0)
        load("w", 1)
        load("s", 0, 256)
        load("q", 0, 512)
        load("q", 512, 1024)
        load("s", 256, 512)
        load("s", 512, 1024)
        tab()
        mkident()
        tw(0)
        cow(0, "S")
        tw(1)
        cow(1, "S")
        il("s", 0, 256, "V")
        qw(0)
        qw(1)
        qz("s", 0, 256)
        il("q", 256, 512, "S")
        il("q", 0, 256, "V")
        st1(0)
        add(0)
        il("q", 768, 1024, "S")
        il("q", 512, 768, "V")
        qk(0)
        qz("q", 0, 512)
        sc(0, 0)
        st1(1)
        qz("q", 512, 1024)
        sc(0, 1)
        il("s", 256, 512, "S")
        il("s", 512, 768, "S")
        mx(0, 0)
        mx(0, 1)
        nmx(0)
        ex(0, 0)
        ex(0, 1)
        qz("s", 256, 512)
        add(1)
        qk(1)
        il("s", 768, 1024, "S")
        st1(2)
        sc(1, 0)
        sc(1, 1)
        add(2)
        qk(2)
        mx(1, 0)
        mx(1, 1)
        nmx(1)
        ex(1, 0)
        ex(1, 1)
        st1(3)
        sc(2, 0)
        sc(2, 1)
        add(3)
        qz("s", 512, 1024)
        rc(0)
        qk(3)
        nm(0, 0, 512, "V")
        nm(0, 512, 1024, "V")
        mx(2, 0)
        mx(2, 1)
        nmx(2)
        ex(2, 0)
        ex(2, 1)
        st1(4)
        sc(3, 0)
        sc(3, 1)
        add(4)
        rc(1)
        qk(4)
        nm(1, 0, 512, "V")
        nm(1, 512, 1024, "V")
        tr(0, 0)
        co(0, 0, "S")
        st(0, 0)
        tr(0, 1)
        co(0, 1, "S")
        st(0, 1)
        mx(3, 0)
        mx(3, 1)
        nmx(3)
        ex(3, 0)
        ex(3, 1)
        st1(5)
        sc(4, 0)
        sc(4, 1)
        add(5)
        rc(2)
        qk(5)
        nm(2, 0, 512, "V")
        nm(2, 512, 1024, "V")
        tr(1, 0)
        co(1, 0, "S")
        st(1, 0)
        tr(1, 1)
        co(1, 1, "S")
        st(1, 1)
        mx(4, 0)
        mx(4, 1)
        nmx(4)
        ex(4, 0)
        ex(4, 1)
        st1(6)
        sc(5, 0)
        sc(5, 1)
        add(6)
        rc(3)
        qk(6)
        nm(3, 0, 512, "V")
        nm(3, 512, 1024, "V")
        tr(2, 0)
        co(2, 0, "S")
        st(2, 0)
        tr(2, 1)
        co(2, 1, "S")
        st(2, 1)
        mx(5, 0)
        mx(5, 1)
        nmx(5)
        ex(5, 0)
        ex(5, 1)
        st1(7)
        sc(6, 0)
        sc(6, 1)
        add(7)
        rc(4)
        qk(7)
        nm(4, 0, 512, "V")
        nm(4, 512, 1024, "V")
        tr(3, 0)
        co(3, 0, "S")
        st(3, 0)
        tr(3, 1)
        co(3, 1, "S")
        st(3, 1)
        mx(6, 0)
        mx(6, 1)
        nmx(6)
        ex(6, 0)
        ex(6, 1)
        sc(7, 0)
        sc(7, 1)
        rc(5)
        nm(5, 0, 512, "V")
        nm(5, 512, 1024, "V")
        tr(4, 0)
        tr(4, 1)
        mx(7, 0)
        mx(7, 1)
        nmx(7)
        ex(7, 0)
        ex(7, 1)
        co(4, 0, "V")
        st(4, 0)
        rc(6)
        nm(6, 0, 512, "V")
        nm(6, 512, 1024, "V")
        co(4, 1, "V")
        st(4, 1)
        tr(5, 0)
        co(5, 0, "S")
        st(5, 0)
        tr(5, 1)
        co(5, 1, "S")
        st(5, 1)
        rc(7)
        nm(7, 0, 256, "V")
        nm(7, 256, 512, "V")
        nm(7, 512, 768, "V")
        nm(7, 768, 1024, "V")
        tr(6, 0)
        co(6, 0, "S")
        st(6, 0)
        tr(7, 0)
        co(7, 0, "V")
        st(7, 0)
        tr(6, 1)
        co(6, 1, "S")
        st(6, 1)
        tr(7, 1)
        co(7, 1, "V")
        st(7, 1)
